import numpy as np
import ml_dtypes


def mxq(x, axis, fmt="e4m3"):
    dtype, down = {"e4m3": (ml_dtypes.float8_e4m3fn, 7), "e5m2": (ml_dtypes.float8_e5m2, 14)}[fmt]
    v = np.moveaxis(np.asarray(x, np.float32).astype(ml_dtypes.bfloat16).astype(np.float64), axis, -1)
    blocks = v.reshape(v.shape[:-1] + (-1, 32))
    amax = np.abs(blocks).max(-1, keepdims=True)
    byte = np.maximum(np.where(amax > 0, np.frexp(amax)[1] - 1 + 127, 0) - down, 1)
    scale = np.exp2(byte - 127.0)
    codes = (blocks / scale).astype(np.float32).astype(dtype).astype(np.float64)
    return np.moveaxis((codes * scale).reshape(v.shape), -1, axis)


WIDE = False


def mx_kscale(k):
    if not WIDE:
        return np.ones(k)
    levels = np.array([10, -10, 5, -5, 0])
    a = np.random.permutation(np.resize(levels, k // 512 * 4)).reshape(k // 512, 4)
    idx = np.arange(k)
    return np.exp2(a[idx // 512, idx % 128 // 32])


BF16 = ml_dtypes.bfloat16


def bf(x):
    return np.asarray(x, np.float32).astype(BF16)


def f64(x):
    return np.asarray(x).astype(np.float64)


B, S, HID, H, KV, D, WIN, QB, KSZ = 4, 2048, 1024, 2, 2, 64, 384, 128, 4
EPS = 1e-5
QD, KVD = H * D, KV * D
C = QD + 2 * KVD


def silu(v):
    return v / (1.0 + np.exp(-v))


def rmsnorm(v, w):
    return v * (1.0 / np.sqrt(np.mean(v * v, axis=-1, keepdims=True) + EPS)) * w


def rotate_half(v):
    h = v.shape[-1] // 2
    return np.concatenate([-v[..., h:], v[..., :h]], axis=-1)


def canon(v, w, b):
    vp = np.pad(v, ((0, 0), (KSZ - 1, 0), (0, 0)))
    y = sum(vp[:, k:k + S, :] * w[:, k] for k in range(KSZ))
    return silu(y + b) + v


def setup_inputs():
    s = mx_kscale(HID)
    sd = 1.0 / np.sqrt(HID)
    inv_freq = 1.0 / (1e6 ** (np.arange(0, D, 2) / D))
    emb = np.concatenate([np.arange(S)[:, None] * inv_freq[None, :]] * 2, axis=-1)
    return {"x": bf(np.random.standard_normal((B, S, HID)) * s),
            "cos": bf(np.cos(emb)), "sin": bf(np.sin(emb)),
            "q_w": bf(np.random.standard_normal((QD, HID)) * sd / s[None, :]),
            "k_w": bf(np.random.standard_normal((KVD, HID)) * sd / s[None, :]),
            "v_w": bf(np.random.standard_normal((KVD, HID)) * sd / s[None, :]),
            "q_norm_w": bf(1.0 + 0.1 * np.random.standard_normal(D)),
            "k_norm_w": bf(1.0 + 0.1 * np.random.standard_normal(D)),
            "canon_w": bf(np.random.standard_normal((C, KSZ)) * 0.5),
            "canon_bias": bf(np.random.standard_normal(C) * 0.3)}


def reference(x, cos, sin, q_w, k_w, v_w, q_norm_w, k_norm_w, canon_w, canon_bias):
    xm = mxq(f64(x), 2, "e4m3")
    q = (xm @ mxq(f64(q_w), 1, "e4m3").T).reshape(B, S, H, D)
    k = (xm @ mxq(f64(k_w), 1, "e4m3").T).reshape(B, S, KV, D)
    v = xm @ mxq(f64(v_w), 1, "e4m3").T
    q = rmsnorm(q, f64(q_norm_w))
    k = rmsnorm(k, f64(k_norm_w))
    u = np.concatenate([q.reshape(B, S, QD), k.reshape(B, S, KVD), v], axis=-1)
    z = canon(u, f64(canon_w), f64(canon_bias))
    q = z[..., :QD].reshape(B, S, H, D)
    k = z[..., QD:QD + KVD].reshape(B, S, KV, D)
    v = z[..., QD + KVD:].reshape(B, S, KV, D)
    c, sn = f64(cos)[:, None, :], f64(sin)[:, None, :]
    return q * c + rotate_half(q) * sn, k * c + rotate_half(k) * sn, v

@@ -1,0 +1,301 @@
+from contextlib import ExitStack
+
+import concourse.mybir as mybir
+from concourse.masks import make_identity
+
+F32 = mybir.dt.float32
+BF16 = mybir.dt.bfloat16
+U32 = mybir.dt.uint32
+U8 = mybir.dt.uint8
+FP8X4 = mybir.dt.float8_e4m3fn_x4
+ALU = mybir.AluOpType
+ACT = mybir.ActivationFunctionType
+
+P = 128
+BATCH, SEQ, HID = 4, 2048, 1024
+HEAD = 64
+HALF = HEAD // 2
+TAPS = 4
+EPS = 1e-5
+PASSES = HID // (4 * P)
+WORD_BLOCKS = HID // (2 * P)
+BLOCK = 512
+SUBS = BLOCK // P
+BLOCKS_PER_SEQ = SEQ // BLOCK
+GROUPS = 3
+QK = 2 * P
+QK_HEADS = QK // HEAD
+HALO = 4
+
+FLOPS = 2 * BATCH * SEQ * HID * GROUPS * P
+
+
+def transpose_words(nc, bank, rows, ident):
+    words = rows.bitcast(F32)
+    for w in range(WORD_BLOCKS):
+        nc.tensor.transpose(bank[:, w, :], words[:, w * P : (w + 1) * P], ident)
+
+
+def words_by_pass(bank):
+    return bank.rearrange("p (g u) r -> p g r u", u=2)
+
+
+def tile_attention_pa_t_kernel(
+    tc, x, cos, sin, q_w, k_w, v_w, q_norm_w, k_norm_w, canon_w, canon_bias, out_0, out_1, out_2
+):
+    nc = tc.nc
+    x_rows = x.flatten_outer_dims()
+    out_rows = [o.rearrange("b s h d -> (b s) (h d)") for o in (out_0, out_1, out_2)]
+
+    with ExitStack() as ctx:
+        consts = ctx.enter_context(tc.tile_pool(name="consts", bufs=1))
+        x_pool = ctx.enter_context(tc.tile_pool(name="x_pool", bufs=3))
+        mx_pool = ctx.enter_context(tc.tile_pool(name="mx_pool", bufs=2))
+        norm_pool = ctx.enter_context(tc.tile_pool(name="norm_pool", bufs=4))
+        u_pool = ctx.enter_context(tc.tile_pool(name="u_pool", bufs=2))
+        conv_pool = ctx.enter_context(tc.tile_pool(name="conv_pool", bufs=2))
+        rope_pool = ctx.enter_context(tc.tile_pool(name="rope_pool", bufs=2))
+        out_pool = ctx.enter_context(tc.tile_pool(name="out_pool", bufs=3))
+        psum = ctx.enter_context(tc.psum_pool(name="psum", bufs=2))
+
+        ident = consts.tile([P, P], F32)
+        make_identity(nc, ident[:])
+
+        w_raw = consts.tile([P, GROUPS, HID], BF16)
+        for grp, w in enumerate((q_w, k_w, v_w)):
+            nc.sync.dma_start(out=w_raw[:, grp, :], in_=w)
+        w_grouped = consts.tile([P, PASSES, GROUPS * P * 4], BF16, align_bytes=64)
+        w_grouped_words = w_grouped[:].bitcast(F32).rearrange("p g (m u) -> p g m u", u=2)
+        for grp in range(GROUPS):
+            w_bank = psum.tile([P, WORD_BLOCKS, P], F32, tag="xt")
+            transpose_words(nc, w_bank, w_raw[:, grp, :], ident[:])
+            nc.scalar.copy(
+                out=w_grouped_words[:, :, grp * P : (grp + 1) * P, :], in_=words_by_pass(w_bank[:])
+            )
+        w_codes = consts.tile([P, PASSES, GROUPS * P], U32, align_bytes=64)
+        w_scales = consts.tile([P, PASSES, GROUPS * P], U8, align_bytes=64)
+        for g in range(PASSES):
+            for lo, hi in ((0, QK), (QK, QK + P)):
+                nc.vector.quantize_mx(
+                    out=w_codes[:, g, lo:hi].bitcast(FP8X4),
+                    scales=w_scales[:, g, lo:hi],
+                    in_=w_grouped[:, g, 4 * lo : 4 * hi],
+                )
+
+        conv_w_bf = consts.tile([P, GROUPS, TAPS], BF16)
+        nc.scalar.dma_start(out=conv_w_bf[:], in_=canon_w.rearrange("(g c) j -> c g j", g=GROUPS))
+        conv_b_bf = consts.tile([P, GROUPS, 1], BF16)
+        nc.scalar.dma_start(
+            out=conv_b_bf[:], in_=canon_bias.rearrange("(g c o) -> c g o", g=GROUPS, o=1)
+        )
+        conv_w = consts.tile([P, GROUPS, TAPS], F32)
+        nc.vector.tensor_copy(out=conv_w[:], in_=conv_w_bf[:])
+        conv_b = consts.tile([P, GROUPS, 1], F32)
+        nc.vector.tensor_copy(out=conv_b[:], in_=conv_b_bf[:])
+        norm_w = consts.tile([P, 2], F32)
+        for col, w in enumerate((q_norm_w, k_norm_w)):
+            norm_w_bf = consts.tile([P, 1], BF16, name="norm_w_bf%d" % col)
+            for head in range(P // HEAD):
+                nc.scalar.dma_start(
+                    out=norm_w_bf[head * HEAD : (head + 1) * HEAD, :],
+                    in_=w.rearrange("(d o) -> d o", o=1),
+                )
+            nc.vector.tensor_copy(out=norm_w[:, col : col + 1], in_=norm_w_bf[:])
+
+        cos_sb = consts.tile([P, SEQ // P, HEAD], BF16)
+        nc.scalar.dma_start(out=cos_sb[:], in_=cos.rearrange("(j p) d -> p j d", p=P))
+        sin_sb = consts.tile([P, SEQ // P, HEAD], BF16)
+        nc.scalar.dma_start(out=sin_sb[:], in_=sin.rearrange("(j p) d -> p j d", p=P))
+        nc.vector.tensor_scalar_mul(
+            out=sin_sb[:, :, 0:HALF], in0=sin_sb[:, :, 0:HALF], scalar1=-1.0
+        )
+
+        minus_half = consts.tile([P, 2 * QK_HEADS], F32)
+        nc.gpsimd.memset(minus_half[:], -0.5)
+
+        u = None
+        for block in range(BATCH * BLOCKS_PER_SEQ):
+            block_in_seq = block % BLOCKS_PER_SEQ
+            tokens = slice(block * BLOCK, (block + 1) * BLOCK)
+            first = HALO + block_in_seq * BLOCK
+
+            if block_in_seq == 0:
+                u = u_pool.tile([P, GROUPS, HALO + SEQ], F32)
+                nc.gpsimd.memset(u[:, :, 0:HALO], 0.0)
+
+            x_raw = x_pool.tile([P, SUBS, HID], BF16)
+            nc.sync.dma_start(
+                out=x_raw[:], in_=x_rows[tokens, :].rearrange("(n p) k -> p n k", p=P)
+            )
+            x_grouped = mx_pool.tile([P, PASSES, BLOCK * 4], BF16, align_bytes=64)
+            x_grouped_words = x_grouped[:].bitcast(F32).rearrange("p g (t u) -> p g t u", u=2)
+            for n in range(SUBS):
+                x_bank = psum.tile([P, WORD_BLOCKS, P], F32, tag="xt")
+                transpose_words(nc, x_bank, x_raw[:, n, :], ident[:])
+                nc.scalar.copy(
+                    out=x_grouped_words[:, :, n * P : (n + 1) * P, :], in_=words_by_pass(x_bank[:])
+                )
+            x_codes = mx_pool.tile([P, PASSES, BLOCK], U32, align_bytes=64)
+            x_scales = mx_pool.tile([P, PASSES, BLOCK], U8, align_bytes=64)
+            nc.vector.quantize_mx(
+                out=x_codes[:].rearrange("p g t -> p (g t)").bitcast(FP8X4),
+                scales=x_scales[:].rearrange("p g t -> p (g t)"),
+                in_=x_grouped[:].rearrange("p g c -> p (g c)"),
+            )
+
+            normed = []
+            for pair in range(SUBS // 2):
+                qk_bank = psum.tile([P, 2, QK], F32, tag="qk")
+                for i in range(2):
+                    t_cols = slice((2 * pair + i) * P, (2 * pair + i + 1) * P)
+                    for g in range(PASSES):
+                        nc.tensor.matmul_mx(
+                            out=qk_bank[:, i, :],
+                            lhsT=x_codes[:, g, t_cols].bitcast(FP8X4),
+                            lhsT_scale=x_scales[:, g, t_cols],
+                            rhs=w_codes[:, g, 0:QK].bitcast(FP8X4),
+                            rhs_scale=w_scales[:, g, 0:QK],
+                            start=(g == 0),
+                            stop=(g == PASSES - 1),
+                        )
+                qk_heads = qk_bank[:].rearrange("p i (h d) -> p (i h) d", d=HEAD)
+                squares = norm_pool.tile([P, 2 * QK_HEADS, HEAD], F32)
+                mean_sq = norm_pool.tile([P, 2 * QK_HEADS], F32)
+                for h in range(2 * QK_HEADS):
+                    nc.scalar.activation(
+                        out=squares[:, h, :],
+                        in_=qk_heads[:, h, :],
+                        func=ACT.Square,
+                        scale=0.125,
+                        accum_out=mean_sq[:, h : h + 1],
+                    )
+                shifted = norm_pool.tile([P, 2 * QK_HEADS], F32)
+                nc.gpsimd.tensor_scalar(
+                    out=shifted[:], in0=mean_sq[:], scalar1=1.0, scalar2=EPS, op0=ALU.mult, op1=ALU.add
+                )
+                rstd = norm_pool.tile([P, 2 * QK_HEADS], F32)
+                nc.gpsimd.tensor_tensor(out=rstd[:], in0=shifted[:], in1=minus_half[:], op=ALU.pow)
+                qk_normed = norm_pool.tile([P, 2, QK], F32)
+                nc.vector.tensor_tensor(
+                    out=qk_normed[:].rearrange("p i (h d) -> p (i h) d", d=HEAD),
+                    in0=qk_heads,
+                    in1=rstd[:].unsqueeze(2).to_broadcast([P, 2 * QK_HEADS, HEAD]),
+                    op=ALU.mult,
+                )
+                normed.append(qk_normed)
+
+            for grp in range(2):
+                u_bank = psum.tile([P, BLOCK], F32, tag="cl")
+                for n in range(SUBS):
+                    nc.tensor.transpose(
+                        u_bank[:, n * P : (n + 1) * P],
+                        normed[n // 2][:, n % 2, grp * P : (grp + 1) * P],
+                        ident[:],
+                    )
+                nc.scalar.activation(
+                    out=u[:, grp, first : first + BLOCK],
+                    in_=u_bank[:],
+                    func=ACT.Copy,
+                    scale=norm_w[:, grp : grp + 1],
+                )
+            v_bank = psum.tile([P, BLOCK], F32, tag="cl")
+            for g in range(PASSES):
+                nc.tensor.matmul_mx(
+                    out=v_bank[:],
+                    lhsT=w_codes[:, g, QK : QK + P].bitcast(FP8X4),
+                    lhsT_scale=w_scales[:, g, QK : QK + P],
+                    rhs=x_codes[:, g, :].bitcast(FP8X4),
+                    rhs_scale=x_scales[:, g, :],
+                    start=(g == 0),
+                    stop=(g == PASSES - 1),
+                )
+            nc.scalar.copy(out=u[:, 2, first : first + BLOCK], in_=v_bank[:])
+
+            conv = conv_pool.tile([P, GROUPS, BLOCK], F32)
+            for grp in range(GROUPS):
+                nc.scalar.activation(
+                    out=conv[:, grp, :],
+                    in_=u[:, grp, first : first + BLOCK],
+                    func=ACT.Copy,
+                    scale=conv_w[:, grp, TAPS - 1 : TAPS],
+                )
+            for tap in range(TAPS - 1):
+                back = TAPS - 1 - tap
+                for grp in range(GROUPS):
+                    nc.vector.scalar_tensor_tensor(
+                        out=conv[:, grp, :],
+                        in0=u[:, grp, first - back : first - back + BLOCK],
+                        scalar=conv_w[:, grp, tap : tap + 1],
+                        in1=conv[:, grp, :],
+                        op0=ALU.mult,
+                        op1=ALU.add,
+                    )
+            gated = conv_pool.tile([P, GROUPS, BLOCK], F32)
+            for grp in range(GROUPS):
+                nc.scalar.activation(
+                    out=gated[:, grp, :], in_=conv[:, grp, :], func=ACT.Silu, bias=conv_b[:, grp, :]
+                )
+
+            def z_to_token_layout(region, grp, n):
+                nc.tensor.matmul(
+                    region,
+                    lhsT=gated[:, grp, n * P : (n + 1) * P],
+                    rhs=ident[:],
+                    is_transpose=True,
+                    start=True,
+                    stop=False,
+                )
+                nc.tensor.matmul(
+                    region,
+                    lhsT=u[:, grp, first + n * P : first + (n + 1) * P],
+                    rhs=ident[:],
+                    is_transpose=True,
+                    start=False,
+                    stop=True,
+                )
+
+            qk_out = out_pool.tile([P, SUBS, QK], F32)
+            for pair in range(SUBS // 2):
+                z_bank = psum.tile([P, 2, QK], F32, tag="zt")
+                for i in range(2):
+                    for grp in range(2):
+                        z_to_token_layout(z_bank[:, i, grp * P : (grp + 1) * P], grp, 2 * pair + i)
+                z = z_bank[:].rearrange("p i (h d) -> p i h d", d=HEAD)
+                j = block_in_seq * SUBS + 2 * pair
+                table_shape = [P, 2, QK_HEADS, HEAD]
+                cos_b = cos_sb[:, j : j + 2, :].unsqueeze(2).to_broadcast(table_shape)
+                sin_b = sin_sb[:, j : j + 2, :].unsqueeze(2).to_broadcast(table_shape)
+                straight = rope_pool.tile(table_shape, F32)
+                nc.vector.tensor_tensor(out=straight[:], in0=z, in1=cos_b, op=ALU.mult)
+                turned = rope_pool.tile(table_shape, F32)
+                nc.vector.tensor_tensor(
+                    out=turned[:, :, :, 0:HALF],
+                    in0=z[:, :, :, HALF:HEAD],
+                    in1=sin_b[:, :, :, 0:HALF],
+                    op=ALU.mult,
+                )
+                nc.vector.tensor_tensor(
+                    out=turned[:, :, :, HALF:HEAD],
+                    in0=z[:, :, :, 0:HALF],
+                    in1=sin_b[:, :, :, HALF:HEAD],
+                    op=ALU.mult,
+                )
+                nc.vector.tensor_tensor(
+                    out=qk_out[:, 2 * pair : 2 * pair + 2, :].rearrange(
+                        "p i (h d) -> p i h d", d=HEAD
+                    ),
+                    in0=straight[:],
+                    in1=turned[:],
+                    op=ALU.add,
+                )
+
+            v_out = out_pool.tile([P, SUBS, P], F32)
+            zv_bank = psum.tile([P, SUBS, P], F32, tag="zt")
+            for n in range(SUBS):
+                z_to_token_layout(zv_bank[:, n, :], 2, n)
+            nc.scalar.copy(out=v_out[:], in_=zv_bank[:])
+
+            for rows, result in zip(out_rows, (qk_out[:, :, 0:P], qk_out[:, :, P:QK], v_out[:])):
+                nc.sync.dma_start(
+                    out=rows[tokens, :].rearrange("(n p) c -> p n c", p=P), in_=result
+                )

@@ -22,10 +22,11 @@ WORD_BLOCKS = HID // (2 * P)
 BLOCK = 512
 SUBS = BLOCK // P
 BLOCKS_PER_SEQ = SEQ // BLOCK
+BLOCKS = BATCH * BLOCKS_PER_SEQ
 GROUPS = 3
 QK = 2 * P
 QK_HEADS = QK // HEAD
-HALO = 4
+HALO = 8
 
 FLOPS = 2 * BATCH * SEQ * HID * GROUPS * P
 
@@ -48,6 +49,7 @@ def tile_attention_pa_t_kernel(
     out_rows = [o.rearrange("b s h d -> (b s) (h d)") for o in (out_0, out_1, out_2)]
 
     with ExitStack() as ctx:
+        ctx.enter_context(tc.manual_schedule())
         consts = ctx.enter_context(tc.tile_pool(name="consts", bufs=1))
         x_pool = ctx.enter_context(tc.tile_pool(name="x_pool", bufs=3))
         mx_pool = ctx.enter_context(tc.tile_pool(name="mx_pool", bufs=2))
@@ -64,6 +66,26 @@ def tile_attention_pa_t_kernel(
         w_raw = consts.tile([P, GROUPS, HID], BF16)
         for grp, w in enumerate((q_w, k_w, v_w)):
             nc.sync.dma_start(out=w_raw[:, grp, :], in_=w)
+        conv_w_bf = consts.tile([P, GROUPS, TAPS], BF16)
+        nc.scalar.dma_start(out=conv_w_bf[:], in_=canon_w.rearrange("(g c) j -> c g j", g=GROUPS))
+        conv_b_bf = consts.tile([P, GROUPS, 1], BF16)
+        nc.scalar.dma_start(
+            out=conv_b_bf[:], in_=canon_bias.rearrange("(g c o) -> c g o", g=GROUPS, o=1)
+        )
+        norm_w_bf = []
+        for w in (q_norm_w, k_norm_w):
+            repeated = consts.tile([P, 1], BF16, name="norm_w_bf%d" % len(norm_w_bf))
+            for head in range(P // HEAD):
+                nc.scalar.dma_start(
+                    out=repeated[head * HEAD : (head + 1) * HEAD, :],
+                    in_=w.rearrange("(d o) -> d o", o=1),
+                )
+            norm_w_bf.append(repeated)
+        cos_sb = consts.tile([P, SEQ // P, HEAD], BF16)
+        nc.scalar.dma_start(out=cos_sb[:], in_=cos.rearrange("(j p) d -> p j d", p=P))
+        sin_sb = consts.tile([P, SEQ // P, HEAD], BF16)
+        nc.scalar.dma_start(out=sin_sb[:], in_=sin.rearrange("(j p) d -> p j d", p=P))
+
         w_grouped = consts.tile([P, PASSES, GROUPS * P * 4], BF16, align_bytes=64)
         w_grouped_words = w_grouped[:].bitcast(F32).rearrange("p g (m u) -> p g m u", u=2)
         for grp in range(GROUPS):
@@ -82,51 +104,41 @@ def tile_attention_pa_t_kernel(
                     in_=w_grouped[:, g, 4 * lo : 4 * hi],
                 )
 
-        conv_w_bf = consts.tile([P, GROUPS, TAPS], BF16)
-        nc.scalar.dma_start(out=conv_w_bf[:], in_=canon_w.rearrange("(g c) j -> c g j", g=GROUPS))
-        conv_b_bf = consts.tile([P, GROUPS, 1], BF16)
-        nc.scalar.dma_start(
-            out=conv_b_bf[:], in_=canon_bias.rearrange("(g c o) -> c g o", g=GROUPS, o=1)
-        )
         conv_w = consts.tile([P, GROUPS, TAPS], F32)
         nc.vector.tensor_copy(out=conv_w[:], in_=conv_w_bf[:])
         conv_b = consts.tile([P, GROUPS, 1], F32)
         nc.vector.tensor_copy(out=conv_b[:], in_=conv_b_bf[:])
         norm_w = consts.tile([P, 2], F32)
-        for col, w in enumerate((q_norm_w, k_norm_w)):
-            norm_w_bf = consts.tile([P, 1], BF16, name="norm_w_bf%d" % col)
-            for head in range(P // HEAD):
-                nc.scalar.dma_start(
-                    out=norm_w_bf[head * HEAD : (head + 1) * HEAD, :],
-                    in_=w.rearrange("(d o) -> d o", o=1),
-                )
-            nc.vector.tensor_copy(out=norm_w[:, col : col + 1], in_=norm_w_bf[:])
-
-        cos_sb = consts.tile([P, SEQ // P, HEAD], BF16)
-        nc.scalar.dma_start(out=cos_sb[:], in_=cos.rearrange("(j p) d -> p j d", p=P))
-        sin_sb = consts.tile([P, SEQ // P, HEAD], BF16)
-        nc.scalar.dma_start(out=sin_sb[:], in_=sin.rearrange("(j p) d -> p j d", p=P))
+        for grp in range(2):
+            nc.vector.tensor_copy(out=norm_w[:, grp : grp + 1], in_=norm_w_bf[grp][:])
         nc.vector.tensor_scalar_mul(
             out=sin_sb[:, :, 0:HALF], in0=sin_sb[:, :, 0:HALF], scalar1=-1.0
         )
-
         minus_half = consts.tile([P, 2 * QK_HEADS], F32)
         nc.gpsimd.memset(minus_half[:], -0.5)
 
-        u = None
-        for block in range(BATCH * BLOCKS_PER_SEQ):
-            block_in_seq = block % BLOCKS_PER_SEQ
-            tokens = slice(block * BLOCK, (block + 1) * BLOCK)
-            first = HALO + block_in_seq * BLOCK
+        kept = {}
 
-            if block_in_seq == 0:
-                u = u_pool.tile([P, GROUPS, HALO + SEQ], F32)
-                nc.gpsimd.memset(u[:, :, 0:HALO], 0.0)
+        def missing(block):
+            return not 0 <= block < BLOCKS
 
+        def first_column(block):
+            return HALO + (block % BLOCKS_PER_SEQ) * BLOCK
+
+        def load_x(block):
+            if missing(block):
+                return
             x_raw = x_pool.tile([P, SUBS, HID], BF16)
             nc.sync.dma_start(
-                out=x_raw[:], in_=x_rows[tokens, :].rearrange("(n p) k -> p n k", p=P)
+                out=x_raw[:],
+                in_=x_rows[block * BLOCK : (block + 1) * BLOCK, :].rearrange("(n p) k -> p n k", p=P),
             )
+            kept["x_raw", block] = x_raw
+
+        def transpose_x(block):
+            if missing(block):
+                return
+            x_raw = kept["x_raw", block]
             x_grouped = mx_pool.tile([P, PASSES, BLOCK * 4], BF16, align_bytes=64)
             x_grouped_words = x_grouped[:].bitcast(F32).rearrange("p g (t u) -> p g t u", u=2)
             for n in range(SUBS):
@@ -135,30 +147,62 @@ def tile_attention_pa_t_kernel(
                 nc.scalar.copy(
                     out=x_grouped_words[:, :, n * P : (n + 1) * P, :], in_=words_by_pass(x_bank[:])
                 )
+            kept["x_grouped", block] = x_grouped
+
+        def quantise_x(block):
+            if missing(block):
+                return
             x_codes = mx_pool.tile([P, PASSES, BLOCK], U32, align_bytes=64)
             x_scales = mx_pool.tile([P, PASSES, BLOCK], U8, align_bytes=64)
             nc.vector.quantize_mx(
                 out=x_codes[:].rearrange("p g t -> p (g t)").bitcast(FP8X4),
                 scales=x_scales[:].rearrange("p g t -> p (g t)"),
-                in_=x_grouped[:].rearrange("p g c -> p (g c)"),
+                in_=kept["x_grouped", block][:].rearrange("p g c -> p (g c)"),
             )
+            kept["x_codes", block] = x_codes
+            kept["x_scales", block] = x_scales
 
-            normed = []
+        def products(block):
+            if missing(block):
+                return
+            x_codes = kept["x_codes", block]
+            x_scales = kept["x_scales", block]
             for pair in range(SUBS // 2):
                 qk_bank = psum.tile([P, 2, QK], F32, tag="qk")
                 for i in range(2):
-                    t_cols = slice((2 * pair + i) * P, (2 * pair + i + 1) * P)
+                    t_lo = (2 * pair + i) * P
                     for g in range(PASSES):
                         nc.tensor.matmul_mx(
                             out=qk_bank[:, i, :],
-                            lhsT=x_codes[:, g, t_cols].bitcast(FP8X4),
-                            lhsT_scale=x_scales[:, g, t_cols],
+                            lhsT=x_codes[:, g, t_lo : t_lo + P].bitcast(FP8X4),
+                            lhsT_scale=x_scales[:, g, t_lo : t_lo + P],
                             rhs=w_codes[:, g, 0:QK].bitcast(FP8X4),
                             rhs_scale=w_scales[:, g, 0:QK],
                             start=(g == 0),
                             stop=(g == PASSES - 1),
                         )
-                qk_heads = qk_bank[:].rearrange("p i (h d) -> p (i h) d", d=HEAD)
+                kept["qk_bank", block, pair] = qk_bank
+            v_bank = psum.tile([P, BLOCK], F32, tag="cl")
+            for g in range(PASSES):
+                nc.tensor.matmul_mx(
+                    out=v_bank[:],
+                    lhsT=w_codes[:, g, QK : QK + P].bitcast(FP8X4),
+                    lhsT_scale=w_scales[:, g, QK : QK + P],
+                    rhs=x_codes[:, g, :].bitcast(FP8X4),
+                    rhs_scale=x_scales[:, g, :],
+                    start=(g == 0),
+                    stop=(g == PASSES - 1),
+                )
+            kept["v_bank", block] = v_bank
+
+        def by_head(two_tiles):
+            return two_tiles.rearrange("p i (h d) -> p (i h) d", d=HEAD)
+
+        def inverse_rms(block):
+            if missing(block):
+                return
+            for pair in range(SUBS // 2):
+                qk_heads = by_head(kept["qk_bank", block, pair][:])
                 squares = norm_pool.tile([P, 2 * QK_HEADS, HEAD], F32)
                 mean_sq = norm_pool.tile([P, 2 * QK_HEADS], F32)
                 for h in range(2 * QK_HEADS):
@@ -175,127 +219,193 @@ def tile_attention_pa_t_kernel(
                 )
                 rstd = norm_pool.tile([P, 2 * QK_HEADS], F32)
                 nc.gpsimd.tensor_tensor(out=rstd[:], in0=shifted[:], in1=minus_half[:], op=ALU.pow)
-                qk_normed = norm_pool.tile([P, 2, QK], F32)
-                nc.vector.tensor_tensor(
-                    out=qk_normed[:].rearrange("p i (h d) -> p (i h) d", d=HEAD),
-                    in0=qk_heads,
-                    in1=rstd[:].unsqueeze(2).to_broadcast([P, 2 * QK_HEADS, HEAD]),
-                    op=ALU.mult,
-                )
-                normed.append(qk_normed)
+                kept["rstd", block, pair] = rstd
 
+        def normalise(block, pair):
+            if missing(block):
+                return
+            qk_normed = norm_pool.tile([P, 2, QK], F32)
+            nc.vector.tensor_tensor(
+                out=by_head(qk_normed[:]),
+                in0=by_head(kept["qk_bank", block, pair][:]),
+                in1=kept["rstd", block, pair][:].unsqueeze(2).to_broadcast([P, 2 * QK_HEADS, HEAD]),
+                op=ALU.mult,
+            )
+            kept["qk_normed", block, pair] = qk_normed
+
+        def u_of(block):
+            seq = block // BLOCKS_PER_SEQ
+            if ("u", seq) not in kept:
+                u = u_pool.tile([P, GROUPS, HALO + SEQ], F32)
+                nc.gpsimd.memset(u[:, :, 0:HALO], 0.0)
+                kept["u", seq] = u
+            return kept["u", seq]
+
+        def copy_v(block):
+            if missing(block):
+                return
+            first = first_column(block)
+            nc.scalar.copy(out=u_of(block)[:, 2, first : first + BLOCK], in_=kept["v_bank", block][:])
+
+        def qk_to_channels(block):
+            if missing(block):
+                return
+            first = first_column(block)
             for grp in range(2):
                 u_bank = psum.tile([P, BLOCK], F32, tag="cl")
                 for n in range(SUBS):
                     nc.tensor.transpose(
                         u_bank[:, n * P : (n + 1) * P],
-                        normed[n // 2][:, n % 2, grp * P : (grp + 1) * P],
+                        kept["qk_normed", block, n // 2][:, n % 2, grp * P : (grp + 1) * P],
                         ident[:],
                     )
                 nc.scalar.activation(
-                    out=u[:, grp, first : first + BLOCK],
+                    out=u_of(block)[:, grp, first : first + BLOCK],
                     in_=u_bank[:],
                     func=ACT.Copy,
                     scale=norm_w[:, grp : grp + 1],
                 )
-            v_bank = psum.tile([P, BLOCK], F32, tag="cl")
-            for g in range(PASSES):
-                nc.tensor.matmul_mx(
-                    out=v_bank[:],
-                    lhsT=w_codes[:, g, QK : QK + P].bitcast(FP8X4),
-                    lhsT_scale=w_scales[:, g, QK : QK + P],
-                    rhs=x_codes[:, g, :].bitcast(FP8X4),
-                    rhs_scale=x_scales[:, g, :],
-                    start=(g == 0),
-                    stop=(g == PASSES - 1),
-                )
-            nc.scalar.copy(out=u[:, 2, first : first + BLOCK], in_=v_bank[:])
 
+        def last_tap(block):
+            if missing(block):
+                return
+            first = first_column(block)
             conv = conv_pool.tile([P, GROUPS, BLOCK], F32)
             for grp in range(GROUPS):
                 nc.scalar.activation(
                     out=conv[:, grp, :],
-                    in_=u[:, grp, first : first + BLOCK],
+                    in_=u_of(block)[:, grp, first : first + BLOCK],
                     func=ACT.Copy,
                     scale=conv_w[:, grp, TAPS - 1 : TAPS],
                 )
+            kept["conv", block] = conv
+
+        def other_taps(block):
+            if missing(block):
+                return
+            conv = kept["conv", block]
             for tap in range(TAPS - 1):
-                back = TAPS - 1 - tap
+                start = first_column(block) - (TAPS - 1 - tap)
                 for grp in range(GROUPS):
                     nc.vector.scalar_tensor_tensor(
                         out=conv[:, grp, :],
-                        in0=u[:, grp, first - back : first - back + BLOCK],
+                        in0=u_of(block)[:, grp, start : start + BLOCK],
                         scalar=conv_w[:, grp, tap : tap + 1],
                         in1=conv[:, grp, :],
                         op0=ALU.mult,
                         op1=ALU.add,
                     )
+
+        def gate(block):
+            if missing(block):
+                return
             gated = conv_pool.tile([P, GROUPS, BLOCK], F32)
             for grp in range(GROUPS):
                 nc.scalar.activation(
-                    out=gated[:, grp, :], in_=conv[:, grp, :], func=ACT.Silu, bias=conv_b[:, grp, :]
+                    out=gated[:, grp, :],
+                    in_=kept["conv", block][:, grp, :],
+                    func=ACT.Silu,
+                    bias=conv_b[:, grp, :],
                 )
+            kept["gated", block] = gated
 
-            def z_to_token_layout(region, grp, n):
-                nc.tensor.matmul(
-                    region,
-                    lhsT=gated[:, grp, n * P : (n + 1) * P],
-                    rhs=ident[:],
-                    is_transpose=True,
-                    start=True,
-                    stop=False,
-                )
-                nc.tensor.matmul(
-                    region,
-                    lhsT=u[:, grp, first + n * P : first + (n + 1) * P],
-                    rhs=ident[:],
-                    is_transpose=True,
-                    start=False,
-                    stop=True,
-                )
+        def z_to_tokens(region, block, grp, n):
+            first = first_column(block)
+            nc.tensor.matmul(
+                region,
+                lhsT=kept["gated", block][:, grp, n * P : (n + 1) * P],
+                rhs=ident[:],
+                is_transpose=True,
+                start=True,
+                stop=False,
+            )
+            nc.tensor.matmul(
+                region,
+                lhsT=u_of(block)[:, grp, first + n * P : first + (n + 1) * P],
+                rhs=ident[:],
+                is_transpose=True,
+                start=False,
+                stop=True,
+            )
 
-            qk_out = out_pool.tile([P, SUBS, QK], F32)
-            for pair in range(SUBS // 2):
-                z_bank = psum.tile([P, 2, QK], F32, tag="zt")
-                for i in range(2):
-                    for grp in range(2):
-                        z_to_token_layout(z_bank[:, i, grp * P : (grp + 1) * P], grp, 2 * pair + i)
-                z = z_bank[:].rearrange("p i (h d) -> p i h d", d=HEAD)
-                j = block_in_seq * SUBS + 2 * pair
-                table_shape = [P, 2, QK_HEADS, HEAD]
-                cos_b = cos_sb[:, j : j + 2, :].unsqueeze(2).to_broadcast(table_shape)
-                sin_b = sin_sb[:, j : j + 2, :].unsqueeze(2).to_broadcast(table_shape)
-                straight = rope_pool.tile(table_shape, F32)
-                nc.vector.tensor_tensor(out=straight[:], in0=z, in1=cos_b, op=ALU.mult)
-                turned = rope_pool.tile(table_shape, F32)
-                nc.vector.tensor_tensor(
-                    out=turned[:, :, :, 0:HALF],
-                    in0=z[:, :, :, HALF:HEAD],
-                    in1=sin_b[:, :, :, 0:HALF],
-                    op=ALU.mult,
-                )
-                nc.vector.tensor_tensor(
-                    out=turned[:, :, :, HALF:HEAD],
-                    in0=z[:, :, :, 0:HALF],
-                    in1=sin_b[:, :, :, HALF:HEAD],
-                    op=ALU.mult,
-                )
-                nc.vector.tensor_tensor(
-                    out=qk_out[:, 2 * pair : 2 * pair + 2, :].rearrange(
-                        "p i (h d) -> p i h d", d=HEAD
-                    ),
-                    in0=straight[:],
-                    in1=turned[:],
-                    op=ALU.add,
-                )
+        def rows_of(out, block):
+            return out[block * BLOCK : (block + 1) * BLOCK, :].rearrange("(n p) c -> p n c", p=P)
 
-            v_out = out_pool.tile([P, SUBS, P], F32)
+        def finish_v(block):
+            if missing(block):
+                return
             zv_bank = psum.tile([P, SUBS, P], F32, tag="zt")
             for n in range(SUBS):
-                z_to_token_layout(zv_bank[:, n, :], 2, n)
+                z_to_tokens(zv_bank[:, n, :], block, 2, n)
+            v_out = out_pool.tile([P, SUBS, P], F32)
             nc.scalar.copy(out=v_out[:], in_=zv_bank[:])
+            nc.sync.dma_start(out=rows_of(out_rows[2], block), in_=v_out[:])
 
-            for rows, result in zip(out_rows, (qk_out[:, :, 0:P], qk_out[:, :, P:QK], v_out[:])):
-                nc.sync.dma_start(
-                    out=rows[tokens, :].rearrange("(n p) c -> p n c", p=P), in_=result
-                )
+        def qk_to_tokens(block, pair):
+            if missing(block):
+                return
+            z_bank = psum.tile([P, 2, QK], F32, tag="zt")
+            for i in range(2):
+                for grp in range(2):
+                    z_to_tokens(z_bank[:, i, grp * P : (grp + 1) * P], block, grp, 2 * pair + i)
+            kept["z_bank", block, pair] = z_bank
+
+        def rotate(block, pair):
+            if missing(block):
+                return
+            if pair == 0:
+                kept["qk_out", block] = out_pool.tile([P, SUBS, QK], F32, name="qk_out")
+            qk_out = kept["qk_out", block]
+            z = kept["z_bank", block, pair][:].rearrange("p i (h d) -> p i h d", d=HEAD)
+            j = (block % BLOCKS_PER_SEQ) * SUBS + 2 * pair
+            table_shape = [P, 2, QK_HEADS, HEAD]
+            cos_b = cos_sb[:, j : j + 2, :].unsqueeze(2).to_broadcast(table_shape)
+            sin_b = sin_sb[:, j : j + 2, :].unsqueeze(2).to_broadcast(table_shape)
+            straight = rope_pool.tile(table_shape, F32)
+            nc.vector.tensor_tensor(out=straight[:], in0=z, in1=cos_b, op=ALU.mult)
+            turned = rope_pool.tile(table_shape, F32)
+            nc.vector.tensor_tensor(
+                out=turned[:, :, :, 0:HALF],
+                in0=z[:, :, :, HALF:HEAD],
+                in1=sin_b[:, :, :, 0:HALF],
+                op=ALU.mult,
+            )
+            nc.vector.tensor_tensor(
+                out=turned[:, :, :, HALF:HEAD],
+                in0=z[:, :, :, 0:HALF],
+                in1=sin_b[:, :, :, HALF:HEAD],
+                op=ALU.mult,
+            )
+            nc.vector.tensor_tensor(
+                out=qk_out[:, 2 * pair : 2 * pair + 2, :].rearrange("p i (h d) -> p i h d", d=HEAD),
+                in0=straight[:],
+                in1=turned[:],
+                op=ALU.add,
+            )
+
+        def store_qk(block):
+            if missing(block):
+                return
+            qk_out = kept["qk_out", block]
+            nc.sync.dma_start(out=rows_of(out_rows[0], block), in_=qk_out[:, :, 0:P])
+            nc.sync.dma_start(out=rows_of(out_rows[1], block), in_=qk_out[:, :, P:QK])
+
+        for r in range(-4, BLOCKS + 2):
+            load_x(r + 4)
+            products(r)
+            inverse_rms(r)
+            finish_v(r - 2)
+            quantise_x(r + 1)
+            other_taps(r - 1)
+            qk_to_tokens(r - 2, 0)
+            normalise(r, 0)
+            copy_v(r)
+            rotate(r - 2, 0)
+            transpose_x(r + 2)
+            normalise(r, 1)
+            qk_to_tokens(r - 2, 1)
+            rotate(r - 2, 1)
+            store_qk(r - 2)
+            gate(r - 1)
+            qk_to_channels(r)
+            last_tap(r)

@@ -390,22 +390,22 @@ def tile_attention_pa_t_kernel(
             nc.sync.dma_start(out=rows_of(out_rows[0], block), in_=qk_out[:, :, 0:P])
             nc.sync.dma_start(out=rows_of(out_rows[1], block), in_=qk_out[:, :, P:QK])
 
-        for r in range(-4, BLOCKS + 2):
+        for r in range(-4, BLOCKS + 3):
             load_x(r + 4)
             products(r)
             inverse_rms(r)
-            finish_v(r - 2)
-            quantise_x(r + 1)
-            other_taps(r - 1)
-            qk_to_tokens(r - 2, 0)
-            normalise(r, 0)
             copy_v(r)
-            rotate(r - 2, 0)
+            qk_to_channels(r - 1)
+            last_tap(r - 1)
+            finish_v(r - 3)
+            quantise_x(r + 1)
+            other_taps(r - 2)
+            qk_to_tokens(r - 3, 0)
+            normalise(r, 0)
+            rotate(r - 3, 0)
             transpose_x(r + 2)
+            qk_to_tokens(r - 3, 1)
             normalise(r, 1)
-            qk_to_tokens(r - 2, 1)
-            rotate(r - 2, 1)
-            store_qk(r - 2)
-            gate(r - 1)
-            qk_to_channels(r)
-            last_tap(r)
+            rotate(r - 3, 1)
+            store_qk(r - 3)
+            gate(r - 2)

@@ -18,11 +18,11 @@ HALF = HEAD // 2
 TAPS = 4
 EPS = 1e-5
 PASSES = HID // (4 * P)
-WORD_BLOCKS = HID // (2 * P)
-BLOCK = 512
-SUBS = BLOCK // P
-BLOCKS_PER_SEQ = SEQ // BLOCK
-BLOCKS = BATCH * BLOCKS_PER_SEQ
+WORD_TILES = HID // (2 * P)
+CHUNK = 256
+SUBS = CHUNK // P
+CHUNKS_PER_SEQ = SEQ // CHUNK
+CHUNKS = BATCH * CHUNKS_PER_SEQ
 GROUPS = 3
 QK = 2 * P
 QK_HEADS = QK // HEAD
@@ -33,7 +33,7 @@ FLOPS = 2 * BATCH * SEQ * HID * GROUPS * P
 
 def transpose_words(nc, bank, rows, ident):
     words = rows.bitcast(F32)
-    for w in range(WORD_BLOCKS):
+    for w in range(WORD_TILES):
         nc.tensor.transpose(bank[:, w, :], words[:, w * P : (w + 1) * P], ident)
 
 
@@ -51,9 +51,9 @@ def tile_attention_pa_t_kernel(
     with ExitStack() as ctx:
         ctx.enter_context(tc.manual_schedule())
         consts = ctx.enter_context(tc.tile_pool(name="consts", bufs=1))
-        x_pool = ctx.enter_context(tc.tile_pool(name="x_pool", bufs=3))
+        x_pool = ctx.enter_context(tc.tile_pool(name="x_pool", bufs=4))
         mx_pool = ctx.enter_context(tc.tile_pool(name="mx_pool", bufs=2))
-        norm_pool = ctx.enter_context(tc.tile_pool(name="norm_pool", bufs=4))
+        norm_pool = ctx.enter_context(tc.tile_pool(name="norm_pool", bufs=3))
         u_pool = ctx.enter_context(tc.tile_pool(name="u_pool", bufs=2))
         conv_pool = ctx.enter_context(tc.tile_pool(name="conv_pool", bufs=2))
         rope_pool = ctx.enter_context(tc.tile_pool(name="rope_pool", bufs=2))
@@ -89,7 +89,7 @@ def tile_attention_pa_t_kernel(
         w_grouped = consts.tile([P, PASSES, GROUPS * P * 4], BF16, align_bytes=64)
         w_grouped_words = w_grouped[:].bitcast(F32).rearrange("p g (m u) -> p g m u", u=2)
         for grp in range(GROUPS):
-            w_bank = psum.tile([P, WORD_BLOCKS, P], F32, tag="xt")
+            w_bank = psum.tile([P, WORD_TILES, P], F32, tag="xt")
             transpose_words(nc, w_bank, w_raw[:, grp, :], ident[:])
             nc.scalar.copy(
                 out=w_grouped_words[:, :, grp * P : (grp + 1) * P, :], in_=words_by_pass(w_bank[:])
@@ -114,75 +114,73 @@ def tile_attention_pa_t_kernel(
         nc.vector.tensor_scalar_mul(
             out=sin_sb[:, :, 0:HALF], in0=sin_sb[:, :, 0:HALF], scalar1=-1.0
         )
-        minus_half = consts.tile([P, 2 * QK_HEADS], F32)
+        minus_half = consts.tile([P, SUBS * QK_HEADS], F32)
         nc.gpsimd.memset(minus_half[:], -0.5)
 
         kept = {}
 
-        def missing(block):
-            return not 0 <= block < BLOCKS
+        def missing(chunk):
+            return not 0 <= chunk < CHUNKS
 
-        def first_column(block):
-            return HALO + (block % BLOCKS_PER_SEQ) * BLOCK
+        def first_column(chunk):
+            return HALO + (chunk % CHUNKS_PER_SEQ) * CHUNK
 
-        def load_x(block):
-            if missing(block):
+        def load_x(chunk):
+            if missing(chunk):
                 return
             x_raw = x_pool.tile([P, SUBS, HID], BF16)
             nc.sync.dma_start(
                 out=x_raw[:],
-                in_=x_rows[block * BLOCK : (block + 1) * BLOCK, :].rearrange("(n p) k -> p n k", p=P),
+                in_=x_rows[chunk * CHUNK : (chunk + 1) * CHUNK, :].rearrange("(n p) k -> p n k", p=P),
             )
-            kept["x_raw", block] = x_raw
+            kept["x_raw", chunk] = x_raw
 
-        def transpose_x(block):
-            if missing(block):
+        def transpose_x(chunk):
+            if missing(chunk):
                 return
-            x_raw = kept["x_raw", block]
-            x_grouped = mx_pool.tile([P, PASSES, BLOCK * 4], BF16, align_bytes=64)
+            x_raw = kept["x_raw", chunk]
+            x_grouped = mx_pool.tile([P, PASSES, CHUNK * 4], BF16, align_bytes=64)
             x_grouped_words = x_grouped[:].bitcast(F32).rearrange("p g (t u) -> p g t u", u=2)
             for n in range(SUBS):
-                x_bank = psum.tile([P, WORD_BLOCKS, P], F32, tag="xt")
+                x_bank = psum.tile([P, WORD_TILES, P], F32, tag="xt")
                 transpose_words(nc, x_bank, x_raw[:, n, :], ident[:])
                 nc.scalar.copy(
                     out=x_grouped_words[:, :, n * P : (n + 1) * P, :], in_=words_by_pass(x_bank[:])
                 )
-            kept["x_grouped", block] = x_grouped
+            kept["x_grouped", chunk] = x_grouped
 
-        def quantise_x(block):
-            if missing(block):
+        def quantise_x(chunk):
+            if missing(chunk):
                 return
-            x_codes = mx_pool.tile([P, PASSES, BLOCK], U32, align_bytes=64)
-            x_scales = mx_pool.tile([P, PASSES, BLOCK], U8, align_bytes=64)
+            x_codes = mx_pool.tile([P, PASSES, CHUNK], U32, align_bytes=64)
+            x_scales = mx_pool.tile([P, PASSES, CHUNK], U8, align_bytes=64)
             nc.vector.quantize_mx(
                 out=x_codes[:].rearrange("p g t -> p (g t)").bitcast(FP8X4),
                 scales=x_scales[:].rearrange("p g t -> p (g t)"),
-                in_=kept["x_grouped", block][:].rearrange("p g c -> p (g c)"),
+                in_=kept["x_grouped", chunk][:].rearrange("p g c -> p (g c)"),
             )
-            kept["x_codes", block] = x_codes
-            kept["x_scales", block] = x_scales
+            kept["x_codes", chunk] = x_codes
+            kept["x_scales", chunk] = x_scales
 
-        def products(block):
-            if missing(block):
+        def products(chunk):
+            if missing(chunk):
                 return
-            x_codes = kept["x_codes", block]
-            x_scales = kept["x_scales", block]
-            for pair in range(SUBS // 2):
-                qk_bank = psum.tile([P, 2, QK], F32, tag="qk")
-                for i in range(2):
-                    t_lo = (2 * pair + i) * P
-                    for g in range(PASSES):
-                        nc.tensor.matmul_mx(
-                            out=qk_bank[:, i, :],
-                            lhsT=x_codes[:, g, t_lo : t_lo + P].bitcast(FP8X4),
-                            lhsT_scale=x_scales[:, g, t_lo : t_lo + P],
-                            rhs=w_codes[:, g, 0:QK].bitcast(FP8X4),
-                            rhs_scale=w_scales[:, g, 0:QK],
-                            start=(g == 0),
-                            stop=(g == PASSES - 1),
-                        )
-                kept["qk_bank", block, pair] = qk_bank
-            v_bank = psum.tile([P, BLOCK], F32, tag="cl")
+            x_codes = kept["x_codes", chunk]
+            x_scales = kept["x_scales", chunk]
+            qk_bank = psum.tile([P, SUBS, QK], F32, tag="qk")
+            for n in range(SUBS):
+                for g in range(PASSES):
+                    nc.tensor.matmul_mx(
+                        out=qk_bank[:, n, :],
+                        lhsT=x_codes[:, g, n * P : (n + 1) * P].bitcast(FP8X4),
+                        lhsT_scale=x_scales[:, g, n * P : (n + 1) * P],
+                        rhs=w_codes[:, g, 0:QK].bitcast(FP8X4),
+                        rhs_scale=w_scales[:, g, 0:QK],
+                        start=(g == 0),
+                        stop=(g == PASSES - 1),
+                    )
+            kept["qk_bank", chunk] = qk_bank
+            v_bank = psum.tile([P, CHUNK], F32, tag="cl")
             for g in range(PASSES):
                 nc.tensor.matmul_mx(
                     out=v_bank[:],
@@ -193,127 +191,127 @@ def tile_attention_pa_t_kernel(
                     start=(g == 0),
                     stop=(g == PASSES - 1),
                 )
-            kept["v_bank", block] = v_bank
+            kept["v_bank", chunk] = v_bank
 
-        def by_head(two_tiles):
-            return two_tiles.rearrange("p i (h d) -> p (i h) d", d=HEAD)
+        def by_head(qk):
+            return qk.rearrange("p n (h d) -> p (n h) d", d=HEAD)
 
-        def inverse_rms(block):
-            if missing(block):
+        def inverse_rms(chunk):
+            if missing(chunk):
                 return
-            for pair in range(SUBS // 2):
-                qk_heads = by_head(kept["qk_bank", block, pair][:])
-                squares = norm_pool.tile([P, 2 * QK_HEADS, HEAD], F32)
-                mean_sq = norm_pool.tile([P, 2 * QK_HEADS], F32)
-                for h in range(2 * QK_HEADS):
-                    nc.scalar.activation(
-                        out=squares[:, h, :],
-                        in_=qk_heads[:, h, :],
-                        func=ACT.Square,
-                        scale=0.125,
-                        accum_out=mean_sq[:, h : h + 1],
-                    )
-                shifted = norm_pool.tile([P, 2 * QK_HEADS], F32)
-                nc.gpsimd.tensor_scalar(
-                    out=shifted[:], in0=mean_sq[:], scalar1=1.0, scalar2=EPS, op0=ALU.mult, op1=ALU.add
+            qk_heads = by_head(kept["qk_bank", chunk][:])
+            squares = norm_pool.tile([P, SUBS * QK_HEADS, HEAD], F32)
+            mean_sq = norm_pool.tile([P, SUBS * QK_HEADS], F32)
+            for h in range(SUBS * QK_HEADS):
+                nc.scalar.activation(
+                    out=squares[:, h, :],
+                    in_=qk_heads[:, h, :],
+                    func=ACT.Square,
+                    scale=0.125,
+                    accum_out=mean_sq[:, h : h + 1],
                 )
-                rstd = norm_pool.tile([P, 2 * QK_HEADS], F32)
-                nc.gpsimd.tensor_tensor(out=rstd[:], in0=shifted[:], in1=minus_half[:], op=ALU.pow)
-                kept["rstd", block, pair] = rstd
+            shifted = norm_pool.tile([P, SUBS * QK_HEADS], F32)
+            nc.gpsimd.tensor_scalar(
+                out=shifted[:], in0=mean_sq[:], scalar1=1.0, scalar2=EPS, op0=ALU.mult, op1=ALU.add
+            )
+            rstd = norm_pool.tile([P, SUBS * QK_HEADS], F32)
+            nc.gpsimd.tensor_tensor(out=rstd[:], in0=shifted[:], in1=minus_half[:], op=ALU.pow)
+            kept["rstd", chunk] = rstd
 
-        def normalise(block, pair):
-            if missing(block):
+        def normalise(chunk):
+            if missing(chunk):
                 return
-            qk_normed = norm_pool.tile([P, 2, QK], F32)
+            qk_normed = norm_pool.tile([P, SUBS, QK], F32)
             nc.vector.tensor_tensor(
                 out=by_head(qk_normed[:]),
-                in0=by_head(kept["qk_bank", block, pair][:]),
-                in1=kept["rstd", block, pair][:].unsqueeze(2).to_broadcast([P, 2 * QK_HEADS, HEAD]),
+                in0=by_head(kept["qk_bank", chunk][:]),
+                in1=kept["rstd", chunk][:].unsqueeze(2).to_broadcast([P, SUBS * QK_HEADS, HEAD]),
                 op=ALU.mult,
             )
-            kept["qk_normed", block, pair] = qk_normed
+            kept["qk_normed", chunk] = qk_normed
 
-        def u_of(block):
-            seq = block // BLOCKS_PER_SEQ
+        def u_of(chunk):
+            seq = chunk // CHUNKS_PER_SEQ
             if ("u", seq) not in kept:
                 u = u_pool.tile([P, GROUPS, HALO + SEQ], F32)
                 nc.gpsimd.memset(u[:, :, 0:HALO], 0.0)
                 kept["u", seq] = u
             return kept["u", seq]
 
-        def copy_v(block):
-            if missing(block):
+        def copy_v(chunk):
+            if missing(chunk):
                 return
-            first = first_column(block)
-            nc.scalar.copy(out=u_of(block)[:, 2, first : first + BLOCK], in_=kept["v_bank", block][:])
+            first = first_column(chunk)
+            nc.scalar.copy(out=u_of(chunk)[:, 2, first : first + CHUNK], in_=kept["v_bank", chunk][:])
 
-        def qk_to_channels(block):
-            if missing(block):
+        def qk_to_channels(chunk):
+            if missing(chunk):
                 return
-            first = first_column(block)
+            first = first_column(chunk)
+            u_bank = psum.tile([P, 2, CHUNK], F32, tag="cl")
             for grp in range(2):
-                u_bank = psum.tile([P, BLOCK], F32, tag="cl")
                 for n in range(SUBS):
                     nc.tensor.transpose(
-                        u_bank[:, n * P : (n + 1) * P],
-                        kept["qk_normed", block, n // 2][:, n % 2, grp * P : (grp + 1) * P],
+                        u_bank[:, grp, n * P : (n + 1) * P],
+                        kept["qk_normed", chunk][:, n, grp * P : (grp + 1) * P],
                         ident[:],
                     )
+            for grp in range(2):
                 nc.scalar.activation(
-                    out=u_of(block)[:, grp, first : first + BLOCK],
-                    in_=u_bank[:],
+                    out=u_of(chunk)[:, grp, first : first + CHUNK],
+                    in_=u_bank[:, grp, :],
                     func=ACT.Copy,
                     scale=norm_w[:, grp : grp + 1],
                 )
 
-        def last_tap(block):
-            if missing(block):
+        def last_tap(chunk):
+            if missing(chunk):
                 return
-            first = first_column(block)
-            conv = conv_pool.tile([P, GROUPS, BLOCK], F32)
+            first = first_column(chunk)
+            conv = conv_pool.tile([P, GROUPS, CHUNK], F32)
             for grp in range(GROUPS):
                 nc.scalar.activation(
                     out=conv[:, grp, :],
-                    in_=u_of(block)[:, grp, first : first + BLOCK],
+                    in_=u_of(chunk)[:, grp, first : first + CHUNK],
                     func=ACT.Copy,
                     scale=conv_w[:, grp, TAPS - 1 : TAPS],
                 )
-            kept["conv", block] = conv
+            kept["conv", chunk] = conv
 
-        def other_taps(block):
-            if missing(block):
+        def other_taps(chunk):
+            if missing(chunk):
                 return
-            conv = kept["conv", block]
+            conv = kept["conv", chunk]
             for tap in range(TAPS - 1):
-                start = first_column(block) - (TAPS - 1 - tap)
+                start = first_column(chunk) - (TAPS - 1 - tap)
                 for grp in range(GROUPS):
                     nc.vector.scalar_tensor_tensor(
                         out=conv[:, grp, :],
-                        in0=u_of(block)[:, grp, start : start + BLOCK],
+                        in0=u_of(chunk)[:, grp, start : start + CHUNK],
                         scalar=conv_w[:, grp, tap : tap + 1],
                         in1=conv[:, grp, :],
                         op0=ALU.mult,
                         op1=ALU.add,
                     )
 
-        def gate(block):
-            if missing(block):
+        def gate(chunk):
+            if missing(chunk):
                 return
-            gated = conv_pool.tile([P, GROUPS, BLOCK], F32)
+            gated = conv_pool.tile([P, GROUPS, CHUNK], F32)
             for grp in range(GROUPS):
                 nc.scalar.activation(
                     out=gated[:, grp, :],
-                    in_=kept["conv", block][:, grp, :],
+                    in_=kept["conv", chunk][:, grp, :],
                     func=ACT.Silu,
                     bias=conv_b[:, grp, :],
                 )
-            kept["gated", block] = gated
+            kept["gated", chunk] = gated
 
-        def z_to_tokens(region, block, grp, n):
-            first = first_column(block)
+        def z_to_tokens(region, chunk, grp, n):
+            first = first_column(chunk)
             nc.tensor.matmul(
                 region,
-                lhsT=kept["gated", block][:, grp, n * P : (n + 1) * P],
+                lhsT=kept["gated", chunk][:, grp, n * P : (n + 1) * P],
                 rhs=ident[:],
                 is_transpose=True,
                 start=True,
@@ -321,46 +319,43 @@ def tile_attention_pa_t_kernel(
             )
             nc.tensor.matmul(
                 region,
-                lhsT=u_of(block)[:, grp, first + n * P : first + (n + 1) * P],
+                lhsT=u_of(chunk)[:, grp, first + n * P : first + (n + 1) * P],
                 rhs=ident[:],
                 is_transpose=True,
                 start=False,
                 stop=True,
             )
 
-        def rows_of(out, block):
-            return out[block * BLOCK : (block + 1) * BLOCK, :].rearrange("(n p) c -> p n c", p=P)
+        def rows_of(out, chunk):
+            return out[chunk * CHUNK : (chunk + 1) * CHUNK, :].rearrange("(n p) c -> p n c", p=P)
 
-        def finish_v(block):
-            if missing(block):
+        def finish_v(chunk):
+            if missing(chunk):
                 return
             zv_bank = psum.tile([P, SUBS, P], F32, tag="zt")
             for n in range(SUBS):
-                z_to_tokens(zv_bank[:, n, :], block, 2, n)
+                z_to_tokens(zv_bank[:, n, :], chunk, 2, n)
             v_out = out_pool.tile([P, SUBS, P], F32)
             nc.scalar.copy(out=v_out[:], in_=zv_bank[:])
-            nc.sync.dma_start(out=rows_of(out_rows[2], block), in_=v_out[:])
+            nc.sync.dma_start(out=rows_of(out_rows[2], chunk), in_=v_out[:])
 
-        def qk_to_tokens(block, pair):
-            if missing(block):
+        def qk_to_tokens(chunk):
+            if missing(chunk):
                 return
-            z_bank = psum.tile([P, 2, QK], F32, tag="zt")
-            for i in range(2):
+            z_bank = psum.tile([P, SUBS, QK], F32, tag="zt")
+            for n in range(SUBS):
                 for grp in range(2):
-                    z_to_tokens(z_bank[:, i, grp * P : (grp + 1) * P], block, grp, 2 * pair + i)
-            kept["z_bank", block, pair] = z_bank
+                    z_to_tokens(z_bank[:, n, grp * P : (grp + 1) * P], chunk, grp, n)
+            kept["z_bank", chunk] = z_bank
 
-        def rotate(block, pair):
-            if missing(block):
+        def rotate(chunk):
+            if missing(chunk):
                 return
-            if pair == 0:
-                kept["qk_out", block] = out_pool.tile([P, SUBS, QK], F32, name="qk_out")
-            qk_out = kept["qk_out", block]
-            z = kept["z_bank", block, pair][:].rearrange("p i (h d) -> p i h d", d=HEAD)
-            j = (block % BLOCKS_PER_SEQ) * SUBS + 2 * pair
-            table_shape = [P, 2, QK_HEADS, HEAD]
-            cos_b = cos_sb[:, j : j + 2, :].unsqueeze(2).to_broadcast(table_shape)
-            sin_b = sin_sb[:, j : j + 2, :].unsqueeze(2).to_broadcast(table_shape)
+            z = kept["z_bank", chunk][:].rearrange("p n (h d) -> p n h d", d=HEAD)
+            j = (chunk % CHUNKS_PER_SEQ) * SUBS
+            table_shape = [P, SUBS, QK_HEADS, HEAD]
+            cos_b = cos_sb[:, j : j + SUBS, :].unsqueeze(2).to_broadcast(table_shape)
+            sin_b = sin_sb[:, j : j + SUBS, :].unsqueeze(2).to_broadcast(table_shape)
             straight = rope_pool.tile(table_shape, F32)
             nc.vector.tensor_tensor(out=straight[:], in0=z, in1=cos_b, op=ALU.mult)
             turned = rope_pool.tile(table_shape, F32)
@@ -376,36 +371,28 @@ def tile_attention_pa_t_kernel(
                 in1=sin_b[:, :, :, HALF:HEAD],
                 op=ALU.mult,
             )
+            qk_out = out_pool.tile([P, SUBS, QK], F32)
             nc.vector.tensor_tensor(
-                out=qk_out[:, 2 * pair : 2 * pair + 2, :].rearrange("p i (h d) -> p i h d", d=HEAD),
+                out=qk_out[:].rearrange("p n (h d) -> p n h d", d=HEAD),
                 in0=straight[:],
                 in1=turned[:],
                 op=ALU.add,
             )
+            nc.sync.dma_start(out=rows_of(out_rows[0], chunk), in_=qk_out[:, :, 0:P])
+            nc.sync.dma_start(out=rows_of(out_rows[1], chunk), in_=qk_out[:, :, P:QK])
 
-        def store_qk(block):
-            if missing(block):
-                return
-            qk_out = kept["qk_out", block]
-            nc.sync.dma_start(out=rows_of(out_rows[0], block), in_=qk_out[:, :, 0:P])
-            nc.sync.dma_start(out=rows_of(out_rows[1], block), in_=qk_out[:, :, P:QK])
-
-        for r in range(-4, BLOCKS + 3):
-            load_x(r + 4)
+        for r in range(-5, CHUNKS + 3):
+            load_x(r + 5)
             products(r)
             inverse_rms(r)
             copy_v(r)
+            quantise_x(r + 1)
+            transpose_x(r + 2)
+            other_taps(r - 2)
+            finish_v(r - 3)
             qk_to_channels(r - 1)
             last_tap(r - 1)
-            finish_v(r - 3)
-            quantise_x(r + 1)
-            other_taps(r - 2)
-            qk_to_tokens(r - 3, 0)
-            normalise(r, 0)
-            rotate(r - 3, 0)
-            transpose_x(r + 2)
-            qk_to_tokens(r - 3, 1)
-            normalise(r, 1)
-            rotate(r - 3, 1)
-            store_qk(r - 3)
             gate(r - 2)
+            qk_to_tokens(r - 3)
+            rotate(r - 3)
+            normalise(r)

@@ -348,7 +348,7 @@ def tile_attention_pa_t_kernel(
                     z_to_tokens(z_bank[:, n, grp * P : (grp + 1) * P], chunk, grp, n)
             kept["z_bank", chunk] = z_bank
 
-        def rotate(chunk):
+        def rotate_products(chunk):
             if missing(chunk):
                 return
             z = kept["z_bank", chunk][:].rearrange("p n (h d) -> p n h d", d=HEAD)
@@ -356,8 +356,6 @@ def tile_attention_pa_t_kernel(
             table_shape = [P, SUBS, QK_HEADS, HEAD]
             cos_b = cos_sb[:, j : j + SUBS, :].unsqueeze(2).to_broadcast(table_shape)
             sin_b = sin_sb[:, j : j + SUBS, :].unsqueeze(2).to_broadcast(table_shape)
-            straight = rope_pool.tile(table_shape, F32)
-            nc.vector.tensor_tensor(out=straight[:], in0=z, in1=cos_b, op=ALU.mult)
             turned = rope_pool.tile(table_shape, F32)
             nc.vector.tensor_tensor(
                 out=turned[:, :, :, 0:HALF],
@@ -371,11 +369,19 @@ def tile_attention_pa_t_kernel(
                 in1=sin_b[:, :, :, HALF:HEAD],
                 op=ALU.mult,
             )
+            straight = rope_pool.tile(table_shape, F32)
+            nc.vector.tensor_tensor(out=straight[:], in0=z, in1=cos_b, op=ALU.mult)
+            kept["turned", chunk] = turned
+            kept["straight", chunk] = straight
+
+        def rotate_sum(chunk):
+            if missing(chunk):
+                return
             qk_out = out_pool.tile([P, SUBS, QK], F32)
             nc.vector.tensor_tensor(
                 out=qk_out[:].rearrange("p n (h d) -> p n h d", d=HEAD),
-                in0=straight[:],
-                in1=turned[:],
+                in0=kept["straight", chunk][:],
+                in1=kept["turned", chunk][:],
                 op=ALU.add,
             )
             nc.sync.dma_start(out=rows_of(out_rows[0], chunk), in_=qk_out[:, :, 0:P])
@@ -394,5 +400,6 @@ def tile_attention_pa_t_kernel(
             last_tap(r - 1)
             gate(r - 2)
             qk_to_tokens(r - 3)
-            rotate(r - 3)
+            rotate_products(r - 3)
             normalise(r)
+            rotate_sum(r - 3)

@@ -167,7 +167,7 @@ def tile_attention_pa_t_kernel(
                 return
             x_codes = kept["x_codes", chunk]
             x_scales = kept["x_scales", chunk]
-            qk_bank = psum.tile([P, SUBS, QK], F32, tag="qk")
+            qk_bank = psum.tile([P, SUBS, QK], F32, tag="qk", bufs=3)
             for n in range(SUBS):
                 for g in range(PASSES):
                     nc.tensor.matmul_mx(
@@ -180,7 +180,7 @@ def tile_attention_pa_t_kernel(
                         stop=(g == PASSES - 1),
                     )
             kept["qk_bank", chunk] = qk_bank
-            v_bank = psum.tile([P, CHUNK], F32, tag="cl")
+            v_bank = psum.tile([P, CHUNK], F32, tag="cl", bufs=1)
             for g in range(PASSES):
                 nc.tensor.matmul_mx(
                     out=v_bank[:],
@@ -248,7 +248,7 @@ def tile_attention_pa_t_kernel(
             if missing(chunk):
                 return
             first = first_column(chunk)
-            u_bank = psum.tile([P, 2, CHUNK], F32, tag="cl")
+            u_bank = psum.tile([P, 2, CHUNK], F32, tag="cl", bufs=1)
             for grp in range(2):
                 for n in range(SUBS):
                     nc.tensor.transpose(
@@ -348,7 +348,7 @@ def tile_attention_pa_t_kernel(
                     z_to_tokens(z_bank[:, n, grp * P : (grp + 1) * P], chunk, grp, n)
             kept["z_bank", chunk] = z_bank
 
-        def rotate_products(chunk):
+        def rotate(chunk):
             if missing(chunk):
                 return
             z = kept["z_bank", chunk][:].rearrange("p n (h d) -> p n h d", d=HEAD)
@@ -356,6 +356,8 @@ def tile_attention_pa_t_kernel(
             table_shape = [P, SUBS, QK_HEADS, HEAD]
             cos_b = cos_sb[:, j : j + SUBS, :].unsqueeze(2).to_broadcast(table_shape)
             sin_b = sin_sb[:, j : j + SUBS, :].unsqueeze(2).to_broadcast(table_shape)
+            straight = rope_pool.tile(table_shape, F32)
+            nc.vector.tensor_tensor(out=straight[:], in0=z, in1=cos_b, op=ALU.mult)
             turned = rope_pool.tile(table_shape, F32)
             nc.vector.tensor_tensor(
                 out=turned[:, :, :, 0:HALF],
@@ -369,37 +371,28 @@ def tile_attention_pa_t_kernel(
                 in1=sin_b[:, :, :, HALF:HEAD],
                 op=ALU.mult,
             )
-            straight = rope_pool.tile(table_shape, F32)
-            nc.vector.tensor_tensor(out=straight[:], in0=z, in1=cos_b, op=ALU.mult)
-            kept["turned", chunk] = turned
-            kept["straight", chunk] = straight
-
-        def rotate_sum(chunk):
-            if missing(chunk):
-                return
             qk_out = out_pool.tile([P, SUBS, QK], F32)
             nc.vector.tensor_tensor(
                 out=qk_out[:].rearrange("p n (h d) -> p n h d", d=HEAD),
-                in0=kept["straight", chunk][:],
-                in1=kept["turned", chunk][:],
+                in0=straight[:],
+                in1=turned[:],
                 op=ALU.add,
             )
             nc.sync.dma_start(out=rows_of(out_rows[0], chunk), in_=qk_out[:, :, 0:P])
             nc.sync.dma_start(out=rows_of(out_rows[1], chunk), in_=qk_out[:, :, P:QK])
 
-        for r in range(-5, CHUNKS + 3):
+        for r in range(-5, CHUNKS + 4):
             load_x(r + 5)
             products(r)
             inverse_rms(r)
             copy_v(r)
             quantise_x(r + 1)
             transpose_x(r + 2)
-            other_taps(r - 2)
-            finish_v(r - 3)
-            qk_to_channels(r - 1)
-            last_tap(r - 1)
-            gate(r - 2)
-            qk_to_tokens(r - 3)
-            rotate_products(r - 3)
-            normalise(r)
-            rotate_sum(r - 3)
+            other_taps(r - 3)
+            normalise(r - 1)
+            finish_v(r - 4)
+            qk_to_channels(r - 2)
+            last_tap(r - 2)
+            gate(r - 3)
+            qk_to_tokens(r - 4)
+            rotate(r - 4)

from contextlib import ExitStack

import concourse.mybir as mybir
from concourse.masks import make_identity

F32 = mybir.dt.float32
BF16 = mybir.dt.bfloat16
U32 = mybir.dt.uint32
U8 = mybir.dt.uint8
FP8X4 = mybir.dt.float8_e4m3fn_x4
ALU = mybir.AluOpType
ACT = mybir.ActivationFunctionType

P = 128
BATCH, SEQ, HID = 4, 2048, 1024
HEAD = 64
HALF = HEAD // 2
TAPS = 4
EPS = 1e-5
PASSES = HID // (4 * P)
WORD_TILES = HID // (2 * P)
CHUNK = 256
SUBS = CHUNK // P
CHUNKS_PER_SEQ = SEQ // CHUNK
CHUNKS = BATCH * CHUNKS_PER_SEQ
GROUPS = 3
QK = 2 * P
QK_HEADS = QK // HEAD
HALO = 8

FLOPS = 2 * BATCH * SEQ * HID * GROUPS * P


def transpose_words(nc, bank, rows, ident):
    words = rows.bitcast(F32)
    for w in range(WORD_TILES):
        nc.tensor.transpose(bank[:, w, :], words[:, w * P : (w + 1) * P], ident)


def words_by_pass(bank):
    return bank.rearrange("p (g u) r -> p g r u", u=2)


def tile_attention_pa_t_kernel(
    tc, x, cos, sin, q_w, k_w, v_w, q_norm_w, k_norm_w, canon_w, canon_bias, out_0, out_1, out_2
):
    nc = tc.nc
    x_rows = x.flatten_outer_dims()
    out_rows = [o.rearrange("b s h d -> (b s) (h d)") for o in (out_0, out_1, out_2)]

    with ExitStack() as ctx:
        ctx.enter_context(tc.manual_schedule())
        consts = ctx.enter_context(tc.tile_pool(name="consts", bufs=1))
        x_pool = ctx.enter_context(tc.tile_pool(name="x_pool", bufs=4))
        mx_pool = ctx.enter_context(tc.tile_pool(name="mx_pool", bufs=2))
        norm_pool = ctx.enter_context(tc.tile_pool(name="norm_pool", bufs=3))
        u_pool = ctx.enter_context(tc.tile_pool(name="u_pool", bufs=2))
        conv_pool = ctx.enter_context(tc.tile_pool(name="conv_pool", bufs=2))
        rope_pool = ctx.enter_context(tc.tile_pool(name="rope_pool", bufs=2))
        out_pool = ctx.enter_context(tc.tile_pool(name="out_pool", bufs=3))
        psum = ctx.enter_context(tc.psum_pool(name="psum", bufs=2))

        ident = consts.tile([P, P], F32)
        make_identity(nc, ident[:])

        w_raw = consts.tile([P, GROUPS, HID], BF16)
        for grp, w in enumerate((q_w, k_w, v_w)):
            nc.sync.dma_start(out=w_raw[:, grp, :], in_=w)
        conv_w_bf = consts.tile([P, GROUPS, TAPS], BF16)
        nc.scalar.dma_start(out=conv_w_bf[:], in_=canon_w.rearrange("(g c) j -> c g j", g=GROUPS))
        conv_b_bf = consts.tile([P, GROUPS, 1], BF16)
        nc.scalar.dma_start(
            out=conv_b_bf[:], in_=canon_bias.rearrange("(g c o) -> c g o", g=GROUPS, o=1)
        )
        norm_w_bf = []
        for w in (q_norm_w, k_norm_w):
            repeated = consts.tile([P, 1], BF16, name="norm_w_bf%d" % len(norm_w_bf))
            for head in range(P // HEAD):
                nc.scalar.dma_start(
                    out=repeated[head * HEAD : (head + 1) * HEAD, :],
                    in_=w.rearrange("(d o) -> d o", o=1),
                )
            norm_w_bf.append(repeated)
        cos_sb = consts.tile([P, SEQ // P, HEAD], BF16)
        nc.scalar.dma_start(out=cos_sb[:], in_=cos.rearrange("(j p) d -> p j d", p=P))
        sin_sb = consts.tile([P, SEQ // P, HEAD], BF16)
        nc.scalar.dma_start(out=sin_sb[:], in_=sin.rearrange("(j p) d -> p j d", p=P))

        w_grouped = consts.tile([P, PASSES, GROUPS * P * 4], BF16, align_bytes=64)
        w_grouped_words = w_grouped[:].bitcast(F32).rearrange("p g (m u) -> p g m u", u=2)
        for grp in range(GROUPS):
            w_bank = psum.tile([P, WORD_TILES, P], F32, tag="xt")
            transpose_words(nc, w_bank, w_raw[:, grp, :], ident[:])
            nc.scalar.copy(
                out=w_grouped_words[:, :, grp * P : (grp + 1) * P, :], in_=words_by_pass(w_bank[:])
            )
        w_codes = consts.tile([P, PASSES, GROUPS * P], U32, align_bytes=64)
        w_scales = consts.tile([P, PASSES, GROUPS * P], U8, align_bytes=64)
        for g in range(PASSES):
            for lo, hi in ((0, QK), (QK, QK + P)):
                nc.vector.quantize_mx(
                    out=w_codes[:, g, lo:hi].bitcast(FP8X4),
                    scales=w_scales[:, g, lo:hi],
                    in_=w_grouped[:, g, 4 * lo : 4 * hi],
                )

        conv_w = consts.tile([P, GROUPS, TAPS], F32)
        nc.vector.tensor_copy(out=conv_w[:], in_=conv_w_bf[:])
        conv_b = consts.tile([P, GROUPS, 1], F32)
        nc.vector.tensor_copy(out=conv_b[:], in_=conv_b_bf[:])
        norm_w = consts.tile([P, 2], F32)
        for grp in range(2):
            nc.vector.tensor_copy(out=norm_w[:, grp : grp + 1], in_=norm_w_bf[grp][:])
        nc.vector.tensor_scalar_mul(
            out=sin_sb[:, :, 0:HALF], in0=sin_sb[:, :, 0:HALF], scalar1=-1.0
        )
        minus_half = consts.tile([P, SUBS * QK_HEADS], F32)
        nc.gpsimd.memset(minus_half[:], -0.5)

        kept = {}

        def missing(chunk):
            return not 0 <= chunk < CHUNKS

        def first_column(chunk):
            return HALO + (chunk % CHUNKS_PER_SEQ) * CHUNK

        def load_x(chunk):
            if missing(chunk):
                return
            x_raw = x_pool.tile([P, SUBS, HID], BF16)
            nc.sync.dma_start(
                out=x_raw[:],
                in_=x_rows[chunk * CHUNK : (chunk + 1) * CHUNK, :].rearrange("(n p) k -> p n k", p=P),
            )
            kept["x_raw", chunk] = x_raw

        def transpose_x(chunk):
            if missing(chunk):
                return
            x_raw = kept["x_raw", chunk]
            x_grouped = mx_pool.tile([P, PASSES, CHUNK * 4], BF16, align_bytes=64)
            x_grouped_words = x_grouped[:].bitcast(F32).rearrange("p g (t u) -> p g t u", u=2)
            for n in range(SUBS):
                x_bank = psum.tile([P, WORD_TILES, P], F32, tag="xt")
                transpose_words(nc, x_bank, x_raw[:, n, :], ident[:])
                nc.scalar.copy(
                    out=x_grouped_words[:, :, n * P : (n + 1) * P, :], in_=words_by_pass(x_bank[:])
                )
            kept["x_grouped", chunk] = x_grouped

        def quantise_x(chunk):
            if missing(chunk):
                return
            x_codes = mx_pool.tile([P, PASSES, CHUNK], U32, align_bytes=64)
            x_scales = mx_pool.tile([P, PASSES, CHUNK], U8, align_bytes=64)
            nc.vector.quantize_mx(
                out=x_codes[:].rearrange("p g t -> p (g t)").bitcast(FP8X4),
                scales=x_scales[:].rearrange("p g t -> p (g t)"),
                in_=kept["x_grouped", chunk][:].rearrange("p g c -> p (g c)"),
            )
            kept["x_codes", chunk] = x_codes
            kept["x_scales", chunk] = x_scales

        def products(chunk):
            if missing(chunk):
                return
            x_codes = kept["x_codes", chunk]
            x_scales = kept["x_scales", chunk]
            qk_bank = psum.tile([P, SUBS, QK], F32, tag="qk", bufs=3)
            for n in range(SUBS):
                for g in range(PASSES):
                    nc.tensor.matmul_mx(
                        out=qk_bank[:, n, :],
                        lhsT=x_codes[:, g, n * P : (n + 1) * P].bitcast(FP8X4),
                        lhsT_scale=x_scales[:, g, n * P : (n + 1) * P],
                        rhs=w_codes[:, g, 0:QK].bitcast(FP8X4),
                        rhs_scale=w_scales[:, g, 0:QK],
                        start=(g == 0),
                        stop=(g == PASSES - 1),
                    )
            kept["qk_bank", chunk] = qk_bank
            v_bank = psum.tile([P, CHUNK], F32, tag="cl", bufs=1)
            for g in range(PASSES):
                nc.tensor.matmul_mx(
                    out=v_bank[:],
                    lhsT=w_codes[:, g, QK : QK + P].bitcast(FP8X4),
                    lhsT_scale=w_scales[:, g, QK : QK + P],
                    rhs=x_codes[:, g, :].bitcast(FP8X4),
                    rhs_scale=x_scales[:, g, :],
                    start=(g == 0),
                    stop=(g == PASSES - 1),
                )
            kept["v_bank", chunk] = v_bank

        def by_head(qk):
            return qk.rearrange("p n (h d) -> p (n h) d", d=HEAD)

        def inverse_rms(chunk):
            if missing(chunk):
                return
            qk_heads = by_head(kept["qk_bank", chunk][:])
            squares = norm_pool.tile([P, SUBS * QK_HEADS, HEAD], F32)
            mean_sq = norm_pool.tile([P, SUBS * QK_HEADS], F32)
            for h in range(SUBS * QK_HEADS):
                nc.scalar.activation(
                    out=squares[:, h, :],
                    in_=qk_heads[:, h, :],
                    func=ACT.Square,
                    scale=0.125,
                    accum_out=mean_sq[:, h : h + 1],
                )
            shifted = norm_pool.tile([P, SUBS * QK_HEADS], F32)
            nc.gpsimd.tensor_scalar(
                out=shifted[:], in0=mean_sq[:], scalar1=1.0, scalar2=EPS, op0=ALU.mult, op1=ALU.add
            )
            rstd = norm_pool.tile([P, SUBS * QK_HEADS], F32)
            nc.gpsimd.tensor_tensor(out=rstd[:], in0=shifted[:], in1=minus_half[:], op=ALU.pow)
            kept["rstd", chunk] = rstd

        def normalise(chunk):
            if missing(chunk):
                return
            qk_normed = norm_pool.tile([P, SUBS, QK], F32)
            nc.vector.tensor_tensor(
                out=by_head(qk_normed[:]),
                in0=by_head(kept["qk_bank", chunk][:]),
                in1=kept["rstd", chunk][:].unsqueeze(2).to_broadcast([P, SUBS * QK_HEADS, HEAD]),
                op=ALU.mult,
            )
            kept["qk_normed", chunk] = qk_normed

        def u_of(chunk):
            seq = chunk // CHUNKS_PER_SEQ
            if ("u", seq) not in kept:
                u = u_pool.tile([P, GROUPS, HALO + SEQ], F32)
                nc.gpsimd.memset(u[:, :, 0:HALO], 0.0)
                kept["u", seq] = u
            return kept["u", seq]

        def copy_v(chunk):
            if missing(chunk):
                return
            first = first_column(chunk)
            nc.scalar.copy(out=u_of(chunk)[:, 2, first : first + CHUNK], in_=kept["v_bank", chunk][:])

        def qk_to_channels(chunk):
            if missing(chunk):
                return
            first = first_column(chunk)
            u_bank = psum.tile([P, 2, CHUNK], F32, tag="cl", bufs=1)
            for grp in range(2):
                for n in range(SUBS):
                    nc.tensor.transpose(
                        u_bank[:, grp, n * P : (n + 1) * P],
                        kept["qk_normed", chunk][:, n, grp * P : (grp + 1) * P],
                        ident[:],
                    )
            for grp in range(2):
                nc.scalar.activation(
                    out=u_of(chunk)[:, grp, first : first + CHUNK],
                    in_=u_bank[:, grp, :],
                    func=ACT.Copy,
                    scale=norm_w[:, grp : grp + 1],
                )

        def last_tap(chunk):
            if missing(chunk):
                return
            first = first_column(chunk)
            conv = conv_pool.tile([P, GROUPS, CHUNK], F32)
            for grp in range(GROUPS):
                nc.scalar.activation(
                    out=conv[:, grp, :],
                    in_=u_of(chunk)[:, grp, first : first + CHUNK],
                    func=ACT.Copy,
                    scale=conv_w[:, grp, TAPS - 1 : TAPS],
                )
            kept["conv", chunk] = conv

        def other_taps(chunk):
            if missing(chunk):
                return
            conv = kept["conv", chunk]
            for tap in range(TAPS - 1):
                start = first_column(chunk) - (TAPS - 1 - tap)
                for grp in range(GROUPS):
                    nc.vector.scalar_tensor_tensor(
                        out=conv[:, grp, :],
                        in0=u_of(chunk)[:, grp, start : start + CHUNK],
                        scalar=conv_w[:, grp, tap : tap + 1],
                        in1=conv[:, grp, :],
                        op0=ALU.mult,
                        op1=ALU.add,
                    )

        def gate(chunk):
            if missing(chunk):
                return
            gated = conv_pool.tile([P, GROUPS, CHUNK], F32)
            for grp in range(GROUPS):
                nc.scalar.activation(
                    out=gated[:, grp, :],
                    in_=kept["conv", chunk][:, grp, :],
                    func=ACT.Silu,
                    bias=conv_b[:, grp, :],
                )
            kept["gated", chunk] = gated

        def z_to_tokens(region, chunk, grp, n):
            first = first_column(chunk)
            nc.tensor.matmul(
                region,
                lhsT=kept["gated", chunk][:, grp, n * P : (n + 1) * P],
                rhs=ident[:],
                is_transpose=True,
                start=True,
                stop=False,
            )
            nc.tensor.matmul(
                region,
                lhsT=u_of(chunk)[:, grp, first + n * P : first + (n + 1) * P],
                rhs=ident[:],
                is_transpose=True,
                start=False,
                stop=True,
            )

        def rows_of(out, chunk):
            return out[chunk * CHUNK : (chunk + 1) * CHUNK, :].rearrange("(n p) c -> p n c", p=P)

        def finish_v(chunk):
            if missing(chunk):
                return
            zv_bank = psum.tile([P, SUBS, P], F32, tag="zt")
            for n in range(SUBS):
                z_to_tokens(zv_bank[:, n, :], chunk, 2, n)
            v_out = out_pool.tile([P, SUBS, P], F32)
            nc.scalar.copy(out=v_out[:], in_=zv_bank[:])
            nc.sync.dma_start(out=rows_of(out_rows[2], chunk), in_=v_out[:])

        def qk_to_tokens(chunk):
            if missing(chunk):
                return
            z_bank = psum.tile([P, SUBS, QK], F32, tag="zt")
            for n in range(SUBS):
                for grp in range(2):
                    z_to_tokens(z_bank[:, n, grp * P : (grp + 1) * P], chunk, grp, n)
            kept["z_bank", chunk] = z_bank

        def rotate(chunk):
            if missing(chunk):
                return
            z = kept["z_bank", chunk][:].rearrange("p n (h d) -> p n h d", d=HEAD)
            j = (chunk % CHUNKS_PER_SEQ) * SUBS
            table_shape = [P, SUBS, QK_HEADS, HEAD]
            cos_b = cos_sb[:, j : j + SUBS, :].unsqueeze(2).to_broadcast(table_shape)
            sin_b = sin_sb[:, j : j + SUBS, :].unsqueeze(2).to_broadcast(table_shape)
            straight = rope_pool.tile(table_shape, F32)
            nc.vector.tensor_tensor(out=straight[:], in0=z, in1=cos_b, op=ALU.mult)
            turned = rope_pool.tile(table_shape, F32)
            nc.vector.tensor_tensor(
                out=turned[:, :, :, 0:HALF],
                in0=z[:, :, :, HALF:HEAD],
                in1=sin_b[:, :, :, 0:HALF],
                op=ALU.mult,
            )
            nc.vector.tensor_tensor(
                out=turned[:, :, :, HALF:HEAD],
                in0=z[:, :, :, 0:HALF],
                in1=sin_b[:, :, :, HALF:HEAD],
                op=ALU.mult,
            )
            qk_out = out_pool.tile([P, SUBS, QK], F32)
            nc.vector.tensor_tensor(
                out=qk_out[:].rearrange("p n (h d) -> p n h d", d=HEAD),
                in0=straight[:],
                in1=turned[:],
                op=ALU.add,
            )
            nc.sync.dma_start(out=rows_of(out_rows[0], chunk), in_=qk_out[:, :, 0:P])
            nc.sync.dma_start(out=rows_of(out_rows[1], chunk), in_=qk_out[:, :, P:QK])

        for r in range(-5, CHUNKS + 4):
            load_x(r + 5)
            products(r)
            inverse_rms(r)
            copy_v(r)
            quantise_x(r + 1)
            transpose_x(r + 2)
            other_taps(r - 3)
            normalise(r - 1)
            finish_v(r - 4)
            qk_to_channels(r - 2)
            last_tap(r - 2)
            gate(r - 3)
            qk_to_tokens(r - 4)
            rotate(r - 4)
